import numpy as np
import ml_dtypes


def mxq(x, axis, fmt="e4m3"):
    dtype, down = {"e4m3": (ml_dtypes.float8_e4m3fn, 7), "e5m2": (ml_dtypes.float8_e5m2, 14)}[fmt]
    v = np.moveaxis(np.asarray(x, np.float32).astype(ml_dtypes.bfloat16).astype(np.float64), axis, -1)
    blocks = v.reshape(v.shape[:-1] + (-1, 32))
    amax = np.abs(blocks).max(-1, keepdims=True)
    byte = np.maximum(np.where(amax > 0, np.frexp(amax)[1] - 1 + 127, 0) - down, 1)
    scale = np.exp2(byte - 127.0)
    codes = (blocks / scale).astype(np.float32).astype(dtype).astype(np.float64)
    return np.moveaxis((codes * scale).reshape(v.shape), -1, axis)


WIDE = False


def mx_kscale(k):
    if not WIDE:
        return np.ones(k)
    levels = np.array([10, -10, 5, -5, 0])
    a = np.random.permutation(np.resize(levels, k // 512 * 4)).reshape(k // 512, 4)
    idx = np.arange(k)
    return np.exp2(a[idx // 512, idx % 128 // 32])


BF16 = ml_dtypes.bfloat16


def bf(x):
    return np.asarray(x, np.float32).astype(BF16)


def f64(x):
    return np.asarray(x).astype(np.float64)


N, D, C, M = 256, 16384, 16, 16


def setup_inputs():
    s = mx_kscale(D)
    return {"x": bf(np.random.standard_normal((N, D)) * s),
            "x_var": bf(0.1 + 4.0 * np.random.standard_normal((N, D)) ** 2),
            "prototypes": bf(np.random.standard_normal((C, M, D)) * 0.5 / np.sqrt(D) / s),
            "proto_var": bf(0.1 + 4.0 * np.random.standard_normal((C, M, D)) ** 2)}


def reference(x, x_var, prototypes, proto_var):
    x, x_var, prototypes, proto_var = f64(x), f64(x_var), f64(prototypes), f64(proto_var)
    lamda = 1.0 / x.shape[-1]
    dot = (mxq(x, 1, "e4m3") @ mxq(prototypes.reshape(C * M, D), 1, "e4m3").T).reshape(N, C, M)
    cross = (mxq(np.sqrt(x_var), 1, "e4m3") @ mxq(np.sqrt(proto_var).reshape(C * M, D), 1, "e4m3").T).reshape(N, C, M)
    w2 = (2.0 - 2.0 * dot
          + lamda * (np.sum(x_var, axis=-1)[:, None, None]
                     + np.sum(proto_var, axis=-1)[None, :, :]
                     - 2.0 * cross))
    return -w2

@@ -1,0 +1,197 @@
+import concourse.mybir as mybir
+from concourse.masks import make_identity
+
+F32 = mybir.dt.float32
+BF16 = mybir.dt.bfloat16
+U32 = mybir.dt.uint32
+U8 = mybir.dt.uint8
+FP8X4 = mybir.dt.float8_e4m3fn_x4
+ACT = mybir.ActivationFunctionType
+ALU = mybir.AluOpType
+AXIS = mybir.AxisListType
+
+P = 128
+ROWS = 256
+ROW_TILES = ROWS // P
+D = 16384
+LAMDA = 1.0 / D
+K_PASS = 4 * P
+N_PASS = D // K_PASS
+CHUNK = 2048
+PASSES_PER_CHUNK = CHUNK // K_PASS
+N_CHUNK = D // CHUNK
+WORDS_PER_PASS = K_PASS // 2
+
+XV, PV, PR, X = 0, 1, 2, 3
+N_OPERANDS = 4
+
+QUANTISE_LAG = 1
+MULTIPLY_LAG = 2
+SUM_LAG = 2
+
+FLOPS = 2 * 2 * ROWS * ROWS * D
+
+
+def tile_probprotoseghead_k_kernel(tc, x, x_var, prototypes, proto_var, out):
+    nc = tc.nc
+
+    def row_tiled(ap):
+        return ap.rearrange("(t p) d -> p t d", p=P)
+
+    sources = {
+        XV: row_tiled(x_var),
+        PV: row_tiled(proto_var.rearrange("c m d -> (c m) d")),
+        PR: row_tiled(prototypes.rearrange("c m d -> (c m) d")),
+        X: row_tiled(x),
+    }
+    out_tiles = out.rearrange("(t p) c m -> t p (c m)", p=P)
+
+    with tc.tile_pool(name="const", bufs=1) as const_pool, tc.tile_pool(
+        name="natural", bufs=3
+    ) as natural_pool, tc.tile_pool(name="grouped", bufs=3) as grouped_pool, tc.tile_pool(
+        name="quantised", bufs=3
+    ) as quantised_pool, tc.tile_pool(name="scratch", bufs=2) as scratch_pool, tc.tile_pool(
+        name="tail", bufs=1
+    ) as tail_pool, tc.psum_pool(name="banks", bufs=1) as bank_pool, tc.psum_pool(
+        name="sums", bufs=1
+    ) as acc_pool, tc.manual_schedule():
+        natural = {}
+        grouped = {}
+        codes = {}
+        scales = {}
+
+        def load_chunk(c, n_parts):
+            natural[c] = {}
+            for i in range(N_OPERANDS):
+                natural[c][i] = natural_pool.tile(
+                    [P, ROW_TILES, CHUNK], BF16, name="natural%d" % i, tag="natural%d" % i
+                )
+            width = CHUNK // n_parts
+            for part in range(n_parts):
+                for i in range(N_OPERANDS):
+                    nc.sync.dma_start(
+                        out=natural[c][i][:, :, part * width : (part + 1) * width],
+                        in_=sources[i][:, :, c * CHUNK + part * width : c * CHUNK + (part + 1) * width],
+                    )
+
+        def transpose_and_group(g):
+            c, q = divmod(g, PASSES_PER_CHUNK)
+            grouped[g] = grouped_pool.tile([P, N_OPERANDS, 4 * ROWS], BF16, name="grouped", align_bytes=64)
+            grouped_words = grouped[g][:].bitcast(F32)
+            banks = {}
+            for i in range(N_OPERANDS):
+                banks[i] = bank_pool.tile([P, 2, ROWS], F32, name="bank%d" % i, tag="bank%d" % i)
+                words = natural[c][i][:].bitcast(F32)
+                for u in range(2):
+                    first = q * WORDS_PER_PASS + u * P
+                    for t in range(ROW_TILES):
+                        nc.tensor.transpose(
+                            banks[i][:, u, t * P : (t + 1) * P], words[:, t, first : first + P], identity[:]
+                        )
+            for i in (XV, PV):
+                nc.scalar.activation(
+                    out=grouped[g][:, i, :].rearrange("p (r u e) -> p r u e", u=2, e=2),
+                    in_=banks[i][:].bitcast(BF16).rearrange("p u (r e) -> p r u e", e=2),
+                    func=ACT.Sqrt,
+                )
+            nc.scalar.copy(
+                out=grouped_words[:, PR, :].rearrange("p (r u) -> p r u", u=2),
+                in_=banks[PR][:].rearrange("p u r -> p r u"),
+            )
+            nc.vector.tensor_copy(
+                out=grouped_words[:, X, :].rearrange("p (r u) -> p r u", u=2),
+                in_=banks[X][:].rearrange("p u r -> p r u"),
+            )
+
+        def quantise(g):
+            codes[g] = quantised_pool.tile([P, N_OPERANDS * ROWS], U32, name="codes", align_bytes=64)
+            scales[g] = quantised_pool.tile([P, N_OPERANDS * ROWS], U8, name="scales", align_bytes=64)
+            nc.vector.quantize_mx(
+                out=codes[g][:].bitcast(FP8X4),
+                scales=scales[g][:],
+                in_=grouped[g][:].rearrange("p i c -> p (i c)"),
+            )
+
+        def multiply(g):
+            for acc, rows_of, columns_of in ((dot, X, PR), (cross, XV, PV)):
+                moving = slice(columns_of * ROWS, (columns_of + 1) * ROWS)
+                for t in range(ROW_TILES):
+                    stationary = slice(rows_of * ROWS + t * P, rows_of * ROWS + (t + 1) * P)
+                    nc.tensor.matmul_mx(
+                        out=acc[t][:],
+                        lhsT=codes[g][:, stationary].bitcast(FP8X4),
+                        lhsT_scale=scales[g][:, stationary],
+                        rhs=codes[g][:, moving].bitcast(FP8X4),
+                        rhs_scale=scales[g][:, moving],
+                        start=(g == 0),
+                        stop=(g == N_PASS - 1),
+                    )
+
+        def sum_row_tile(n):
+            c, j = divmod(n, 2 * ROW_TILES)
+            i, t = divmod(j, ROW_TILES)
+            half = CHUNK // 2
+            pair_sums = scratch_pool.tile([P, half], F32, name="pair_sums")
+            nc.vector.scalar_tensor_tensor(
+                out=pair_sums[:],
+                in0=natural[c][i][:, t, 0:half],
+                scalar=1.0,
+                in1=natural[c][i][:, t, half:CHUNK],
+                op0=ALU.mult,
+                op1=ALU.add,
+                accum_out=partial[:, j * N_CHUNK + c : j * N_CHUNK + c + 1],
+            )
+
+        identity = const_pool.tile([P, P], F32, name="identity")
+        make_identity(nc, identity[:])
+        partial = const_pool.tile([P, 2 * ROW_TILES * N_CHUNK], F32, name="partial")
+        dot = [acc_pool.tile([P, ROWS], F32, name="dot%d" % t) for t in range(ROW_TILES)]
+        cross = [acc_pool.tile([P, ROWS], F32, name="cross%d" % t) for t in range(ROW_TILES)]
+
+        load_chunk(0, PASSES_PER_CHUNK)
+        load_chunk(1, 1)
+
+        for step in range(N_PASS + MULTIPLY_LAG):
+            c, q = divmod(step, PASSES_PER_CHUNK)
+            if q == SUM_LAG and c + 2 < N_CHUNK:
+                load_chunk(c + 2, 1)
+            if step < N_PASS:
+                transpose_and_group(step)
+            if 0 <= step - QUANTISE_LAG < N_PASS:
+                quantise(step - QUANTISE_LAG)
+            if step >= SUM_LAG:
+                sum_row_tile(step - SUM_LAG)
+            if step >= MULTIPLY_LAG:
+                multiply(step - MULTIPLY_LAG)
+
+        totals = tail_pool.tile([P, 2 * ROW_TILES], F32, name="totals")
+        nc.vector.tensor_reduce(
+            out=totals[:], in_=partial[:].rearrange("p (j c) -> p j c", c=N_CHUNK), axis=AXIS.X, op=ALU.add
+        )
+        row_term = tail_pool.tile([P, ROW_TILES], F32, name="row_term")
+        nc.vector.tensor_scalar(
+            out=row_term[:], in0=totals[:, 0:ROW_TILES], scalar1=-LAMDA, scalar2=-2.0, op0=ALU.mult, op1=ALU.add
+        )
+        proto_sums = bank_pool.tile([P, ROWS], F32, name="proto_sums", tag="bank%d" % X)
+        for t in range(ROW_TILES):
+            nc.tensor.matmul(
+                out=proto_sums[:, t * P : (t + 1) * P],
+                lhsT=totals[:, ROW_TILES + t : ROW_TILES + t + 1].to_broadcast([P, P]),
+                rhs=identity[:],
+                start=True,
+                stop=True,
+            )
+        for t in range(ROW_TILES):
+            base = tail_pool.tile([P, ROWS], F32, name="base%d" % t)
+            nc.scalar.activation(
+                out=base[:], in_=proto_sums[:], func=ACT.Identity, bias=row_term[:, t : t + 1], scale=-LAMDA
+            )
+            with_dot = tail_pool.tile([P, ROWS], F32, name="with_dot%d" % t)
+            nc.vector.scalar_tensor_tensor(
+                out=with_dot[:], in0=dot[t][:], scalar=2.0, in1=base[:], op0=ALU.mult, op1=ALU.add
+            )
+            result = tail_pool.tile([P, ROWS], F32, name="result%d" % t)
+            nc.vector.scalar_tensor_tensor(
+                out=result[:], in0=cross[t][:], scalar=2.0 * LAMDA, in1=with_dot[:], op0=ALU.mult, op1=ALU.add
+            )
+            nc.sync.dma_start(out=out_tiles[t], in_=result[:])

@@ -69,10 +69,11 @@ def tile_probprotoseghead_k_kernel(tc, x, x_var, prototypes, proto_var, out):
             width = CHUNK // n_parts
             for part in range(n_parts):
                 for i in range(N_OPERANDS):
-                    nc.sync.dma_start(
-                        out=natural[c][i][:, :, part * width : (part + 1) * width],
-                        in_=sources[i][:, :, c * CHUNK + part * width : c * CHUNK + (part + 1) * width],
-                    )
+                    for t in range(ROW_TILES):
+                        nc.sync.dma_start(
+                            out=natural[c][i][:, t, part * width : (part + 1) * width],
+                            in_=sources[i][:, t, c * CHUNK + part * width : c * CHUNK + (part + 1) * width],
+                        )
 
         def transpose_and_group(g):
             c, q = divmod(g, PASSES_PER_CHUNK)
@@ -168,10 +169,6 @@ def tile_probprotoseghead_k_kernel(tc, x, x_var, prototypes, proto_var, out):
         nc.vector.tensor_reduce(
             out=totals[:], in_=partial[:].rearrange("p (j c) -> p j c", c=N_CHUNK), axis=AXIS.X, op=ALU.add
         )
-        row_term = tail_pool.tile([P, ROW_TILES], F32, name="row_term")
-        nc.vector.tensor_scalar(
-            out=row_term[:], in0=totals[:, 0:ROW_TILES], scalar1=-LAMDA, scalar2=-2.0, op0=ALU.mult, op1=ALU.add
-        )
         proto_sums = bank_pool.tile([P, ROWS], F32, name="proto_sums", tag="bank%d" % X)
         for t in range(ROW_TILES):
             nc.tensor.matmul(
@@ -181,17 +178,23 @@ def tile_probprotoseghead_k_kernel(tc, x, x_var, prototypes, proto_var, out):
                 start=True,
                 stop=True,
             )
+        row_term = tail_pool.tile([P, ROW_TILES], F32, name="row_term")
+        nc.vector.tensor_scalar(
+            out=row_term[:], in0=totals[:, 0:ROW_TILES], scalar1=-LAMDA, scalar2=-2.0, op0=ALU.mult, op1=ALU.add
+        )
+        with_cross = {}
         for t in range(ROW_TILES):
-            base = tail_pool.tile([P, ROWS], F32, name="base%d" % t)
-            nc.scalar.activation(
-                out=base[:], in_=proto_sums[:], func=ACT.Identity, bias=row_term[:, t : t + 1], scale=-LAMDA
-            )
             with_dot = tail_pool.tile([P, ROWS], F32, name="with_dot%d" % t)
-            nc.vector.scalar_tensor_tensor(
-                out=with_dot[:], in0=dot[t][:], scalar=2.0, in1=base[:], op0=ALU.mult, op1=ALU.add
+            nc.scalar.activation(
+                out=with_dot[:], in_=dot[t][:], func=ACT.Identity, bias=row_term[:, t : t + 1], scale=2.0
             )
+            with_cross[t] = tail_pool.tile([P, ROWS], F32, name="with_cross%d" % t)
+            nc.vector.scalar_tensor_tensor(
+                out=with_cross[t][:], in0=cross[t][:], scalar=2.0 * LAMDA, in1=with_dot[:], op0=ALU.mult, op1=ALU.add
+            )
+        for t in range(ROW_TILES):
             result = tail_pool.tile([P, ROWS], F32, name="result%d" % t)
             nc.vector.scalar_tensor_tensor(
-                out=result[:], in0=cross[t][:], scalar=2.0 * LAMDA, in1=with_dot[:], op0=ALU.mult, op1=ALU.add
+                out=result[:], in0=proto_sums[:], scalar=-LAMDA, in1=with_cross[t][:], op0=ALU.mult, op1=ALU.add
             )
             nc.sync.dma_start(out=out_tiles[t], in_=result[:])

@@ -27,7 +27,9 @@ N_OPERANDS = 4
 
 QUANTISE_LAG = 1
 MULTIPLY_LAG = 2
-SUM_LAG = 2
+SUMS_PER_CHUNK = 2 * ROW_TILES
+N_SUMS = SUMS_PER_CHUNK * N_CHUNK
+SUM_LEAD = 2
 
 FLOPS = 2 * 2 * ROWS * ROWS * D
 
@@ -66,9 +68,12 @@ def tile_probprotoseghead_k_kernel(tc, x, x_var, prototypes, proto_var, out):
                 natural[c][i] = natural_pool.tile(
                     [P, ROW_TILES, CHUNK], BF16, name="natural%d" % i, tag="natural%d" % i
                 )
+            for i in (XV, PV):
+                for t in range(ROW_TILES):
+                    nc.sync.dma_start(out=natural[c][i][:, t, :], in_=sources[i][:, t, c * CHUNK : (c + 1) * CHUNK])
             width = CHUNK // n_parts
             for part in range(n_parts):
-                for i in range(N_OPERANDS):
+                for i in (PR, X):
                     for t in range(ROW_TILES):
                         nc.sync.dma_start(
                             out=natural[c][i][:, t, part * width : (part + 1) * width],
@@ -129,7 +134,7 @@ def tile_probprotoseghead_k_kernel(tc, x, x_var, prototypes, proto_var, out):
                     )
 
         def sum_row_tile(n):
-            c, j = divmod(n, 2 * ROW_TILES)
+            c, j = divmod(n, SUMS_PER_CHUNK)
             i, t = divmod(j, ROW_TILES)
             half = CHUNK // 2
             pair_sums = scratch_pool.tile([P, half], F32, name="pair_sums")
@@ -145,23 +150,25 @@ def tile_probprotoseghead_k_kernel(tc, x, x_var, prototypes, proto_var, out):
 
         identity = const_pool.tile([P, P], F32, name="identity")
         make_identity(nc, identity[:])
-        partial = const_pool.tile([P, 2 * ROW_TILES * N_CHUNK], F32, name="partial")
+        partial = const_pool.tile([P, N_SUMS], F32, name="partial")
         dot = [acc_pool.tile([P, ROWS], F32, name="dot%d" % t) for t in range(ROW_TILES)]
         cross = [acc_pool.tile([P, ROWS], F32, name="cross%d" % t) for t in range(ROW_TILES)]
 
         load_chunk(0, PASSES_PER_CHUNK)
         load_chunk(1, 1)
+        for n in range(SUMS_PER_CHUNK):
+            sum_row_tile(n)
 
         for step in range(N_PASS + MULTIPLY_LAG):
             c, q = divmod(step, PASSES_PER_CHUNK)
-            if q == SUM_LAG and c + 2 < N_CHUNK:
+            if q == 0 and c + 2 < N_CHUNK:
                 load_chunk(c + 2, 1)
             if step < N_PASS:
                 transpose_and_group(step)
             if 0 <= step - QUANTISE_LAG < N_PASS:
                 quantise(step - QUANTISE_LAG)
-            if step >= SUM_LAG:
-                sum_row_tile(step - SUM_LAG)
+            if SUMS_PER_CHUNK <= step + SUM_LEAD < N_SUMS:
+                sum_row_tile(step + SUM_LEAD)
             if step >= MULTIPLY_LAG:
                 multiply(step - MULTIPLY_LAG)
 

@@ -15,6 +15,7 @@ ROWS = 256
 ROW_TILES = ROWS // P
 D = 16384
 LAMDA = 1.0 / D
+ROOT_SCALE = 2.0**-14
 K_PASS = 4 * P
 N_PASS = D // K_PASS
 CHUNK = 2048
@@ -54,7 +55,7 @@ def tile_probprotoseghead_k_kernel(tc, x, x_var, prototypes, proto_var, out):
         name="quantised", bufs=3
     ) as quantised_pool, tc.tile_pool(name="scratch", bufs=2) as scratch_pool, tc.tile_pool(
         name="tail", bufs=1
-    ) as tail_pool, tc.psum_pool(name="banks", bufs=1) as bank_pool, tc.psum_pool(
+    ) as tail_pool, tc.psum_pool(name="banks", bufs=6) as bank_pool, tc.psum_pool(
         name="sums", bufs=1
     ) as acc_pool, tc.manual_schedule():
         natural = {}
@@ -80,13 +81,13 @@ def tile_probprotoseghead_k_kernel(tc, x, x_var, prototypes, proto_var, out):
                             in_=sources[i][:, t, c * CHUNK + part * width : c * CHUNK + (part + 1) * width],
                         )
 
-        def transpose_and_group(g):
+        def transpose_and_group(g, copy_prototypes):
             c, q = divmod(g, PASSES_PER_CHUNK)
             grouped[g] = grouped_pool.tile([P, N_OPERANDS, 4 * ROWS], BF16, name="grouped", align_bytes=64)
             grouped_words = grouped[g][:].bitcast(F32)
             banks = {}
             for i in range(N_OPERANDS):
-                banks[i] = bank_pool.tile([P, 2, ROWS], F32, name="bank%d" % i, tag="bank%d" % i)
+                banks[i] = bank_pool.tile([P, 2, ROWS], F32, name="bank", tag="bank")
                 words = natural[c][i][:].bitcast(F32)
                 for u in range(2):
                     first = q * WORDS_PER_PASS + u * P
@@ -99,8 +100,9 @@ def tile_probprotoseghead_k_kernel(tc, x, x_var, prototypes, proto_var, out):
                     out=grouped[g][:, i, :].rearrange("p (r u e) -> p r u e", u=2, e=2),
                     in_=banks[i][:].bitcast(BF16).rearrange("p u (r e) -> p r u e", e=2),
                     func=ACT.Sqrt,
+                    scale=ROOT_SCALE,
                 )
-            nc.scalar.copy(
+            copy_prototypes(
                 out=grouped_words[:, PR, :].rearrange("p (r u) -> p r u", u=2),
                 in_=banks[PR][:].rearrange("p u r -> p r u"),
             )
@@ -119,7 +121,7 @@ def tile_probprotoseghead_k_kernel(tc, x, x_var, prototypes, proto_var, out):
             )
 
         def multiply(g):
-            for acc, rows_of, columns_of in ((dot, X, PR), (cross, XV, PV)):
+            for rows_of, columns_of in ((XV, PV), (X, PR)):
                 moving = slice(columns_of * ROWS, (columns_of + 1) * ROWS)
                 for t in range(ROW_TILES):
                     stationary = slice(rows_of * ROWS + t * P, rows_of * ROWS + (t + 1) * P)
@@ -129,8 +131,8 @@ def tile_probprotoseghead_k_kernel(tc, x, x_var, prototypes, proto_var, out):
                         lhsT_scale=scales[g][:, stationary],
                         rhs=codes[g][:, moving].bitcast(FP8X4),
                         rhs_scale=scales[g][:, moving],
-                        start=(g == 0),
-                        stop=(g == N_PASS - 1),
+                        start=(g == 0 and rows_of == XV),
+                        stop=(g == N_PASS - 1 and rows_of == X),
                     )
 
         def sum_row_tile(n):
@@ -148,60 +150,73 @@ def tile_probprotoseghead_k_kernel(tc, x, x_var, prototypes, proto_var, out):
                 accum_out=partial[:, j * N_CHUNK + c : j * N_CHUNK + c + 1],
             )
 
+        def total_sums():
+            nc.vector.tensor_reduce(
+                out=totals[:], in_=partial[:].rearrange("p (j c) -> p j c", c=N_CHUNK), axis=AXIS.X, op=ALU.add
+            )
+            nc.vector.tensor_scalar(
+                out=row_term[:], in0=totals[:, 0:ROW_TILES], scalar1=-LAMDA, scalar2=-2.0, op0=ALU.mult, op1=ALU.add
+            )
+
+        def spread_proto_sums():
+            proto_sums = bank_pool.tile([P, ROWS], F32, name="proto_sums", tag="bank")
+            for t in range(ROW_TILES):
+                nc.tensor.matmul(
+                    out=proto_sums[:, t * P : (t + 1) * P],
+                    lhsT=totals[:, ROW_TILES + t : ROW_TILES + t + 1].to_broadcast([P, P]),
+                    rhs=identity[:],
+                    start=True,
+                    stop=True,
+                )
+            return proto_sums
+
+        def make_bases(proto_sums):
+            for t in range(ROW_TILES):
+                nc.vector.tensor_scalar(
+                    out=base[t][:],
+                    in0=proto_sums[:],
+                    scalar1=-LAMDA,
+                    scalar2=row_term[:, t : t + 1],
+                    op0=ALU.mult,
+                    op1=ALU.add,
+                )
+
         identity = const_pool.tile([P, P], F32, name="identity")
         make_identity(nc, identity[:])
         partial = const_pool.tile([P, N_SUMS], F32, name="partial")
-        dot = [acc_pool.tile([P, ROWS], F32, name="dot%d" % t) for t in range(ROW_TILES)]
-        cross = [acc_pool.tile([P, ROWS], F32, name="cross%d" % t) for t in range(ROW_TILES)]
+        totals = tail_pool.tile([P, 2 * ROW_TILES], F32, name="totals")
+        row_term = tail_pool.tile([P, ROW_TILES], F32, name="row_term")
+        base = [tail_pool.tile([P, ROWS], F32, name="base%d" % t) for t in range(ROW_TILES)]
+        acc = [acc_pool.tile([P, ROWS], F32, name="acc%d" % t) for t in range(ROW_TILES)]
 
         load_chunk(0, PASSES_PER_CHUNK)
         load_chunk(1, 1)
         for n in range(SUMS_PER_CHUNK):
             sum_row_tile(n)
 
+        last_sum = N_SUMS - SUM_LEAD - 1
         for step in range(N_PASS + MULTIPLY_LAG):
             c, q = divmod(step, PASSES_PER_CHUNK)
             if q == 0 and c + 2 < N_CHUNK:
                 load_chunk(c + 2, 1)
             if step < N_PASS:
-                transpose_and_group(step)
+                transpose_and_group(step, nc.scalar.copy if step <= last_sum else nc.vector.tensor_copy)
             if 0 <= step - QUANTISE_LAG < N_PASS:
                 quantise(step - QUANTISE_LAG)
             if SUMS_PER_CHUNK <= step + SUM_LEAD < N_SUMS:
                 sum_row_tile(step + SUM_LEAD)
+            if step == last_sum + 1:
+                total_sums()
+            if step == last_sum + 2:
+                make_bases(proto_sums)
             if step >= MULTIPLY_LAG:
                 multiply(step - MULTIPLY_LAG)
+            if step == last_sum + 1:
+                proto_sums = spread_proto_sums()
 
-        totals = tail_pool.tile([P, 2 * ROW_TILES], F32, name="totals")
-        nc.vector.tensor_reduce(
-            out=totals[:], in_=partial[:].rearrange("p (j c) -> p j c", c=N_CHUNK), axis=AXIS.X, op=ALU.add
-        )
-        proto_sums = bank_pool.tile([P, ROWS], F32, name="proto_sums", tag="bank%d" % X)
-        for t in range(ROW_TILES):
-            nc.tensor.matmul(
-                out=proto_sums[:, t * P : (t + 1) * P],
-                lhsT=totals[:, ROW_TILES + t : ROW_TILES + t + 1].to_broadcast([P, P]),
-                rhs=identity[:],
-                start=True,
-                stop=True,
-            )
-        row_term = tail_pool.tile([P, ROW_TILES], F32, name="row_term")
-        nc.vector.tensor_scalar(
-            out=row_term[:], in0=totals[:, 0:ROW_TILES], scalar1=-LAMDA, scalar2=-2.0, op0=ALU.mult, op1=ALU.add
-        )
-        with_cross = {}
-        for t in range(ROW_TILES):
-            with_dot = tail_pool.tile([P, ROWS], F32, name="with_dot%d" % t)
-            nc.scalar.activation(
-                out=with_dot[:], in_=dot[t][:], func=ACT.Identity, bias=row_term[:, t : t + 1], scale=2.0
-            )
-            with_cross[t] = tail_pool.tile([P, ROWS], F32, name="with_cross%d" % t)
-            nc.vector.scalar_tensor_tensor(
-                out=with_cross[t][:], in0=cross[t][:], scalar=2.0 * LAMDA, in1=with_dot[:], op0=ALU.mult, op1=ALU.add
-            )
         for t in range(ROW_TILES):
             result = tail_pool.tile([P, ROWS], F32, name="result%d" % t)
             nc.vector.scalar_tensor_tensor(
-                out=result[:], in0=proto_sums[:], scalar=-LAMDA, in1=with_cross[t][:], op0=ALU.mult, op1=ALU.add
+                out=result[:], in0=acc[t][:], scalar=2.0, in1=base[t][:], op0=ALU.mult, op1=ALU.add
             )
             nc.sync.dma_start(out=out_tiles[t], in_=result[:])

@@ -18,19 +18,31 @@ LAMDA = 1.0 / D
 ROOT_SCALE = 2.0**-14
 K_PASS = 4 * P
 N_PASS = D // K_PASS
-CHUNK = 2048
-PASSES_PER_CHUNK = CHUNK // K_PASS
-N_CHUNK = D // CHUNK
 WORDS_PER_PASS = K_PASS // 2
 
 XV, PV, PR, X = 0, 1, 2, 3
 N_OPERANDS = 4
+LEAD = 2
+SUM_TAG, SUM_BUFS = "block_sums", 1
+ORDER = [XV, X, PV, PR]
+BANKS = {XV: 1, PV: 1, PR: 2, X: 1}
+
+OFFSET = {XV: 0, PV: 0, PR: LEAD, X: LEAD}
+N_STEP = N_PASS + LEAD
+
+WIDTHS = [512] * 4 + [1024] * 14
+FIRST_COLUMN = [sum(WIDTHS[:i]) for i in range(len(WIDTHS))]
+N_PIECE = len(WIDTHS)
+PIECE_BUFS = 7
 
 QUANTISE_LAG = 1
 MULTIPLY_LAG = 2
-SUMS_PER_CHUNK = 2 * ROW_TILES
-N_SUMS = SUMS_PER_CHUNK * N_CHUNK
-SUM_LEAD = 2
+SUM_GROUPS = [[0], [1], [2, 3]] + [[i, i + 1] for i in range(4, N_PIECE, 2)]
+N_GROUP = len(SUM_GROUPS)
+SUMS_PER_GROUP = 2 * ROW_TILES
+TENSOR_GROUPS = [4, 5, 6, 7, 8, 9]
+SUMS_BEGIN, SUMS_END = 2, 30
+EARLY_GROUPS = 2
 
 FLOPS = 2 * 2 * ROWS * ROWS * D
 
@@ -50,116 +62,133 @@ def tile_probprotoseghead_k_kernel(tc, x, x_var, prototypes, proto_var, out):
     out_tiles = out.rearrange("(t p) c m -> t p (c m)", p=P)
 
     with tc.tile_pool(name="const", bufs=1) as const_pool, tc.tile_pool(
-        name="natural", bufs=3
-    ) as natural_pool, tc.tile_pool(name="grouped", bufs=3) as grouped_pool, tc.tile_pool(
-        name="quantised", bufs=3
-    ) as quantised_pool, tc.tile_pool(name="scratch", bufs=2) as scratch_pool, tc.tile_pool(
-        name="tail", bufs=1
-    ) as tail_pool, tc.psum_pool(name="banks", bufs=6) as bank_pool, tc.psum_pool(
-        name="sums", bufs=1
-    ) as acc_pool, tc.manual_schedule():
+        name="natural", bufs=PIECE_BUFS
+    ) as natural_pool, tc.tile_pool(
+        name="grouped", bufs=3
+    ) as grouped_pool, tc.tile_pool(name="quantised", bufs=3) as quantised_pool, tc.tile_pool(
+        name="scratch", bufs=2
+    ) as scratch_pool, tc.tile_pool(name="tail", bufs=1) as tail_pool, tc.psum_pool(
+        name="banks", bufs=1
+    ) as bank_pool, tc.psum_pool(name="sums", bufs=1) as acc_pool, tc.manual_schedule():
         natural = {}
         grouped = {}
         codes = {}
         scales = {}
 
-        def load_chunk(c, n_parts):
-            natural[c] = {}
-            for i in range(N_OPERANDS):
-                natural[c][i] = natural_pool.tile(
-                    [P, ROW_TILES, CHUNK], BF16, name="natural%d" % i, tag="natural%d" % i
-                )
-            for i in (XV, PV):
-                for t in range(ROW_TILES):
-                    nc.sync.dma_start(out=natural[c][i][:, t, :], in_=sources[i][:, t, c * CHUNK : (c + 1) * CHUNK])
-            width = CHUNK // n_parts
-            for part in range(n_parts):
-                for i in (PR, X):
-                    for t in range(ROW_TILES):
-                        nc.sync.dma_start(
-                            out=natural[c][i][:, t, part * width : (part + 1) * width],
-                            in_=sources[i][:, t, c * CHUNK + part * width : c * CHUNK + (part + 1) * width],
-                        )
+        def load_piece(i, i_piece):
+            width, first = WIDTHS[i_piece], FIRST_COLUMN[i_piece]
+            natural[i, i_piece] = natural_pool.tile([P, ROW_TILES, width], BF16, name="natural%d" % i, tag="natural%d" % i)
+            nc.sync.dma_start(out=natural[i, i_piece][:], in_=sources[i][:, :, first : first + width])
 
-        def transpose_and_group(g, copy_prototypes):
-            c, q = divmod(g, PASSES_PER_CHUNK)
-            grouped[g] = grouped_pool.tile([P, N_OPERANDS, 4 * ROWS], BF16, name="grouped", align_bytes=64)
-            grouped_words = grouped[g][:].bitcast(F32)
+        def piece_of(column):
+            return max(i for i in range(N_PIECE) if FIRST_COLUMN[i] <= column)
+
+        def operands_of(step):
+            return [i for i in range(N_OPERANDS) if 0 <= step - OFFSET[i] < N_PASS]
+
+        def transpose_and_group(step):
+            grouped[step] = grouped_pool.tile([P, N_OPERANDS, 4 * ROWS], BF16, name="grouped", align_bytes=64)
+            grouped_words = grouped[step][:].bitcast(F32)
             banks = {}
-            for i in range(N_OPERANDS):
-                banks[i] = bank_pool.tile([P, 2, ROWS], F32, name="bank", tag="bank")
-                words = natural[c][i][:].bitcast(F32)
+            for i in [i for i in ORDER if i in operands_of(step)]:
+                column = (step - OFFSET[i]) * K_PASS
+                i_piece = piece_of(column)
+                first_word = (column - FIRST_COLUMN[i_piece]) // 2
+                banks[i] = bank_pool.tile([P, 2, ROWS], F32, name="bank%d" % i, tag="bank%d" % i, bufs=BANKS[i])
+                words = natural[i, i_piece][:].bitcast(F32)
                 for u in range(2):
-                    first = q * WORDS_PER_PASS + u * P
+                    first = first_word + u * P
                     for t in range(ROW_TILES):
                         nc.tensor.transpose(
                             banks[i][:, u, t * P : (t + 1) * P], words[:, t, first : first + P], identity[:]
                         )
-            for i in (XV, PV):
-                nc.scalar.activation(
-                    out=grouped[g][:, i, :].rearrange("p (r u e) -> p r u e", u=2, e=2),
-                    in_=banks[i][:].bitcast(BF16).rearrange("p u (r e) -> p r u e", e=2),
-                    func=ACT.Sqrt,
-                    scale=ROOT_SCALE,
-                )
-            copy_prototypes(
-                out=grouped_words[:, PR, :].rearrange("p (r u) -> p r u", u=2),
-                in_=banks[PR][:].rearrange("p u r -> p r u"),
-            )
-            nc.vector.tensor_copy(
-                out=grouped_words[:, X, :].rearrange("p (r u) -> p r u", u=2),
-                in_=banks[X][:].rearrange("p u r -> p r u"),
-            )
+            for i in operands_of(step):
+                if i in (XV, PV):
+                    nc.scalar.activation(
+                        out=grouped[step][:, i, :].rearrange("p (r u e) -> p r u e", u=2, e=2),
+                        in_=banks[i][:].bitcast(BF16).rearrange("p u (r e) -> p r u e", e=2),
+                        func=ACT.Sqrt,
+                        scale=ROOT_SCALE,
+                    )
+                else:
+                    copy = nc.scalar.copy if i == PR else nc.vector.tensor_copy
+                    copy(
+                        out=grouped_words[:, i, :].rearrange("p (r u) -> p r u", u=2),
+                        in_=banks[i][:].rearrange("p u r -> p r u"),
+                    )
 
-        def quantise(g):
-            codes[g] = quantised_pool.tile([P, N_OPERANDS * ROWS], U32, name="codes", align_bytes=64)
-            scales[g] = quantised_pool.tile([P, N_OPERANDS * ROWS], U8, name="scales", align_bytes=64)
+        def quantise(step):
+            codes[step] = quantised_pool.tile([P, N_OPERANDS * ROWS], U32, name="codes", align_bytes=64)
+            scales[step] = quantised_pool.tile([P, N_OPERANDS * ROWS], U8, name="scales", align_bytes=64)
+            first, last = operands_of(step)[0], operands_of(step)[-1]
+            words = slice(first * ROWS, (last + 1) * ROWS)
             nc.vector.quantize_mx(
-                out=codes[g][:].bitcast(FP8X4),
-                scales=scales[g][:],
-                in_=grouped[g][:].rearrange("p i c -> p (i c)"),
+                out=codes[step][:, words].bitcast(FP8X4),
+                scales=scales[step][:, words],
+                in_=grouped[step][:, first : last + 1, :].rearrange("p i c -> p (i c)"),
             )
 
-        def multiply(g):
+        def multiply(step):
             for rows_of, columns_of in ((XV, PV), (X, PR)):
+                if rows_of not in operands_of(step):
+                    continue
                 moving = slice(columns_of * ROWS, (columns_of + 1) * ROWS)
                 for t in range(ROW_TILES):
                     stationary = slice(rows_of * ROWS + t * P, rows_of * ROWS + (t + 1) * P)
                     nc.tensor.matmul_mx(
                         out=acc[t][:],
-                        lhsT=codes[g][:, stationary].bitcast(FP8X4),
-                        lhsT_scale=scales[g][:, stationary],
-                        rhs=codes[g][:, moving].bitcast(FP8X4),
-                        rhs_scale=scales[g][:, moving],
-                        start=(g == 0 and rows_of == XV),
-                        stop=(g == N_PASS - 1 and rows_of == X),
+                        lhsT=codes[step][:, stationary].bitcast(FP8X4),
+                        lhsT_scale=scales[step][:, stationary],
+                        rhs=codes[step][:, moving].bitcast(FP8X4),
+                        rhs_scale=scales[step][:, moving],
+                        start=(step == 0),
+                        stop=(step == N_STEP - 1),
                     )
 
         def sum_row_tile(n):
-            c, j = divmod(n, SUMS_PER_CHUNK)
+            i_group, j = divmod(n, SUMS_PER_GROUP)
             i, t = divmod(j, ROW_TILES)
-            half = CHUNK // 2
-            pair_sums = scratch_pool.tile([P, half], F32, name="pair_sums")
-            nc.vector.scalar_tensor_tensor(
-                out=pair_sums[:],
-                in0=natural[c][i][:, t, 0:half],
-                scalar=1.0,
-                in1=natural[c][i][:, t, half:CHUNK],
-                op0=ALU.mult,
-                op1=ALU.add,
-                accum_out=partial[:, j * N_CHUNK + c : j * N_CHUNK + c + 1],
-            )
+            total = partial[:, j * N_GROUP + i_group : j * N_GROUP + i_group + 1]
+            pieces = SUM_GROUPS[i_group]
+            width = WIDTHS[pieces[0]]
+            if n in tensor_sums:
+                block_sums = bank_pool.tile([P, P], F32, name="block_sums", tag=SUM_TAG, bufs=SUM_BUFS)
+                blocks = [(i_piece, b) for i_piece in pieces for b in range(width // P)]
+                for n_block, (i_piece, b) in enumerate(blocks):
+                    nc.tensor.matmul(
+                        out=block_sums[:],
+                        lhsT=identity_bf16[:],
+                        rhs=natural[i, i_piece][:, t, b * P : (b + 1) * P],
+                        start=(n_block == 0),
+                        stop=(n_block == len(blocks) - 1),
+                    )
+                nc.vector.tensor_reduce(out=total, in_=block_sums[:], axis=AXIS.X, op=ALU.add)
+            else:
+                if len(pieces) == 2:
+                    parts = [natural[i, i_piece][:, t, :] for i_piece in pieces]
+                else:
+                    parts = [natural[i, pieces[0]][:, t, h * width // 2 : (h + 1) * width // 2] for h in range(2)]
+                pair_sums = scratch_pool.tile([P, len(pieces) * width // 2], F32, name="pair_sums")
+                nc.vector.scalar_tensor_tensor(
+                    out=pair_sums[:],
+                    in0=parts[0],
+                    scalar=1.0,
+                    in1=parts[1],
+                    op0=ALU.mult,
+                    op1=ALU.add,
+                    accum_out=total,
+                )
 
         def total_sums():
             nc.vector.tensor_reduce(
-                out=totals[:], in_=partial[:].rearrange("p (j c) -> p j c", c=N_CHUNK), axis=AXIS.X, op=ALU.add
+                out=totals[:], in_=partial[:].rearrange("p (j c) -> p j c", c=N_GROUP), axis=AXIS.X, op=ALU.add
             )
             nc.vector.tensor_scalar(
                 out=row_term[:], in0=totals[:, 0:ROW_TILES], scalar1=-LAMDA, scalar2=-2.0, op0=ALU.mult, op1=ALU.add
             )
 
         def spread_proto_sums():
-            proto_sums = bank_pool.tile([P, ROWS], F32, name="proto_sums", tag="bank")
+            proto_sums = bank_pool.tile([P, ROWS], F32, name="proto_sums", tag=SUM_TAG, bufs=SUM_BUFS)
             for t in range(ROW_TILES):
                 nc.tensor.matmul(
                     out=proto_sums[:, t * P : (t + 1) * P],
@@ -183,35 +212,61 @@ def tile_probprotoseghead_k_kernel(tc, x, x_var, prototypes, proto_var, out):
 
         identity = const_pool.tile([P, P], F32, name="identity")
         make_identity(nc, identity[:])
-        partial = const_pool.tile([P, N_SUMS], F32, name="partial")
+        identity_bf16 = const_pool.tile([P, P], BF16, name="identity_bf16")
+        make_identity(nc, identity_bf16[:])
+        partial = const_pool.tile([P, SUMS_PER_GROUP * N_GROUP], F32, name="partial")
         totals = tail_pool.tile([P, 2 * ROW_TILES], F32, name="totals")
         row_term = tail_pool.tile([P, ROW_TILES], F32, name="row_term")
         base = [tail_pool.tile([P, ROWS], F32, name="base%d" % t) for t in range(ROW_TILES)]
         acc = [acc_pool.tile([P, ROWS], F32, name="acc%d" % t) for t in range(ROW_TILES)]
 
-        load_chunk(0, PASSES_PER_CHUNK)
-        load_chunk(1, 1)
-        for n in range(SUMS_PER_CHUNK):
-            sum_row_tile(n)
+        tensor_sums = {i_group * SUMS_PER_GROUP + i_group % SUMS_PER_GROUP for i_group in TENSOR_GROUPS}
 
-        last_sum = N_SUMS - SUM_LEAD - 1
-        for step in range(N_PASS + MULTIPLY_LAG):
-            c, q = divmod(step, PASSES_PER_CHUNK)
-            if q == 0 and c + 2 < N_CHUNK:
-                load_chunk(c + 2, 1)
-            if step < N_PASS:
-                transpose_and_group(step, nc.scalar.copy if step <= last_sum else nc.vector.tensor_copy)
-            if 0 <= step - QUANTISE_LAG < N_PASS:
+        loads = sorted(
+            ((i, i_piece) for i in range(N_OPERANDS) for i_piece in range(N_PIECE)),
+            key=lambda load: (FIRST_COLUMN[load[1]] // K_PASS + OFFSET[load[0]], load[0]),
+        )
+        n_load = 0
+        n_sum = 0
+        columns_summed = 0
+        for step in range(N_STEP + MULTIPLY_LAG):
+            while n_load < len(loads):
+                i, i_piece = loads[n_load]
+                oldest = i_piece - PIECE_BUFS
+                if oldest >= 0:
+                    i_group = [k for k in range(N_GROUP) if oldest in SUM_GROUPS[k]][0]
+                    if FIRST_COLUMN[oldest + 1] > (step - OFFSET[i]) * K_PASS:
+                        break
+                    if i in (XV, PV) and n_sum < (i_group + 1) * SUMS_PER_GROUP:
+                        break
+                load_piece(i, i_piece)
+                n_load += 1
+            sums = []
+            while n_sum < SUMS_PER_GROUP * N_GROUP and (
+                n_sum < SUMS_PER_GROUP * min(step + 1, EARLY_GROUPS)
+                or columns_summed * (SUMS_END - SUMS_BEGIN) < D * SUMS_PER_GROUP * (step + 1 - SUMS_BEGIN)
+            ):
+                sums.append(n_sum)
+                pieces = SUM_GROUPS[n_sum // SUMS_PER_GROUP]
+                columns_summed += len(pieces) * WIDTHS[pieces[0]]
+                n_sum += 1
+            if step == 0:
+                for n in sums:
+                    sum_row_tile(n)
+            if step < N_STEP:
+                transpose_and_group(step)
+            if 0 <= step - QUANTISE_LAG < N_STEP:
                 quantise(step - QUANTISE_LAG)
-            if SUMS_PER_CHUNK <= step + SUM_LEAD < N_SUMS:
-                sum_row_tile(step + SUM_LEAD)
-            if step == last_sum + 1:
+            if step > 0:
+                for n in sums:
+                    sum_row_tile(n)
+            if step == SUMS_END:
                 total_sums()
-            if step == last_sum + 2:
+            if step == SUMS_END + 1:
                 make_bases(proto_sums)
             if step >= MULTIPLY_LAG:
                 multiply(step - MULTIPLY_LAG)
-            if step == last_sum + 1:
+            if step == SUMS_END:
                 proto_sums = spread_proto_sums()
 
         for t in range(ROW_TILES):

@@ -42,6 +42,7 @@ N_GROUP = len(SUM_GROUPS)
 SUMS_PER_GROUP = 2 * ROW_TILES
 TENSOR_GROUPS = [4, 5, 6, 7, 8, 9]
 SUMS_BEGIN, SUMS_END = 2, 30
+SPREAD = 1
 EARLY_GROUPS = 2
 
 FLOPS = 2 * 2 * ROWS * ROWS * D
@@ -224,7 +225,7 @@ def tile_probprotoseghead_k_kernel(tc, x, x_var, prototypes, proto_var, out):
 
         loads = sorted(
             ((i, i_piece) for i in range(N_OPERANDS) for i_piece in range(N_PIECE)),
-            key=lambda load: (FIRST_COLUMN[load[1]] // K_PASS + OFFSET[load[0]], load[0]),
+            key=lambda load: (FIRST_COLUMN[load[1]] // K_PASS + OFFSET[load[0]], ORDER.index(load[0])),
         )
         n_load = 0
         n_sum = 0
@@ -262,11 +263,11 @@ def tile_probprotoseghead_k_kernel(tc, x, x_var, prototypes, proto_var, out):
                     sum_row_tile(n)
             if step == SUMS_END:
                 total_sums()
-            if step == SUMS_END + 1:
+            if step == SUMS_END + SPREAD + 1:
                 make_bases(proto_sums)
             if step >= MULTIPLY_LAG:
                 multiply(step - MULTIPLY_LAG)
-            if step == SUMS_END:
+            if step == SUMS_END + SPREAD:
                 proto_sums = spread_proto_sums()
 
         for t in range(ROW_TILES):

@@ -36,12 +36,14 @@ N_PIECE = len(WIDTHS)
 PIECE_BUFS = 7
 
 QUANTISE_LAG = 1
+BURST = 1
 MULTIPLY_LAG = 2
 SUM_GROUPS = [[0], [1], [2, 3]] + [[i, i + 1] for i in range(4, N_PIECE, 2)]
 N_GROUP = len(SUM_GROUPS)
 SUMS_PER_GROUP = 2 * ROW_TILES
-TENSOR_GROUPS = [4, 5, 6, 7, 8, 9]
-SUMS_BEGIN, SUMS_END = 2, 30
+TENSOR_GROUPS = [3, 4, 5, 6, 7, 8]
+REDLAG = -1
+SUMS_BEGIN, SUMS_END = 1, 31
 SPREAD = 1
 EARLY_GROUPS = 2
 
@@ -153,17 +155,7 @@ def tile_probprotoseghead_k_kernel(tc, x, x_var, prototypes, proto_var, out):
             pieces = SUM_GROUPS[i_group]
             width = WIDTHS[pieces[0]]
             if n in tensor_sums:
-                block_sums = bank_pool.tile([P, P], F32, name="block_sums", tag=SUM_TAG, bufs=SUM_BUFS)
-                blocks = [(i_piece, b) for i_piece in pieces for b in range(width // P)]
-                for n_block, (i_piece, b) in enumerate(blocks):
-                    nc.tensor.matmul(
-                        out=block_sums[:],
-                        lhsT=identity_bf16[:],
-                        rhs=natural[i, i_piece][:, t, b * P : (b + 1) * P],
-                        start=(n_block == 0),
-                        stop=(n_block == len(blocks) - 1),
-                    )
-                nc.vector.tensor_reduce(out=total, in_=block_sums[:], axis=AXIS.X, op=ALU.add)
+                nc.vector.tensor_reduce(out=total, in_=block_sums[n][:], axis=AXIS.X, op=ALU.add)
             else:
                 if len(pieces) == 2:
                     parts = [natural[i, i_piece][:, t, :] for i_piece in pieces]
@@ -178,6 +170,23 @@ def tile_probprotoseghead_k_kernel(tc, x, x_var, prototypes, proto_var, out):
                     op0=ALU.mult,
                     op1=ALU.add,
                     accum_out=total,
+                )
+
+        def add_blocks(n, g):
+            k, j = divmod(n, SUMS_PER_GROUP)
+            i, t = divmod(j, ROW_TILES)
+            i_piece = piece_of(g * K_PASS)
+            if g * K_PASS == FIRST_COLUMN[SUM_GROUPS[k][0]]:
+                block_sums[n] = bank_pool.tile([P, P], F32, name="block_sums", tag=SUM_TAG, bufs=SUM_BUFS)
+            for b in range(K_PASS // P):
+                first = g * K_PASS - FIRST_COLUMN[i_piece] + b * P
+                last_column = FIRST_COLUMN[i_piece] + first + P
+                nc.tensor.matmul(
+                    out=block_sums[n][:],
+                    lhsT=identity_bf16[:],
+                    rhs=natural[i, i_piece][:, t, first : first + P],
+                    start=(first + FIRST_COLUMN[i_piece] == FIRST_COLUMN[SUM_GROUPS[k][0]]),
+                    stop=(last_column == FIRST_COLUMN[SUM_GROUPS[k][-1]] + WIDTHS[SUM_GROUPS[k][-1]]),
                 )
 
         def total_sums():
@@ -227,6 +236,9 @@ def tile_probprotoseghead_k_kernel(tc, x, x_var, prototypes, proto_var, out):
             ((i, i_piece) for i in range(N_OPERANDS) for i_piece in range(N_PIECE)),
             key=lambda load: (FIRST_COLUMN[load[1]] // K_PASS + OFFSET[load[0]], ORDER.index(load[0])),
         )
+        block_sums = {}
+        todo = [n for n in range(SUMS_PER_GROUP * N_GROUP) if n not in tensor_sums]
+        all_columns = sum(len(SUM_GROUPS[n // SUMS_PER_GROUP]) * WIDTHS[SUM_GROUPS[n // SUMS_PER_GROUP][0]] for n in todo)
         n_load = 0
         n_sum = 0
         columns_summed = 0
@@ -238,24 +250,31 @@ def tile_probprotoseghead_k_kernel(tc, x, x_var, prototypes, proto_var, out):
                     i_group = [k for k in range(N_GROUP) if oldest in SUM_GROUPS[k]][0]
                     if FIRST_COLUMN[oldest + 1] > (step - OFFSET[i]) * K_PASS:
                         break
-                    if i in (XV, PV) and n_sum < (i_group + 1) * SUMS_PER_GROUP:
+                    if i in (XV, PV) and n_sum < len(todo) and todo[n_sum] < (i_group + 1) * SUMS_PER_GROUP:
                         break
                 load_piece(i, i_piece)
                 n_load += 1
             sums = []
-            while n_sum < SUMS_PER_GROUP * N_GROUP and (
-                n_sum < SUMS_PER_GROUP * min(step + 1, EARLY_GROUPS)
-                or columns_summed * (SUMS_END - SUMS_BEGIN) < D * SUMS_PER_GROUP * (step + 1 - SUMS_BEGIN)
+            while n_sum < len(todo) and (
+                todo[n_sum] < SUMS_PER_GROUP * min(step + 1, EARLY_GROUPS)
+                or columns_summed * (SUMS_END - SUMS_BEGIN) < all_columns * (step + 1 - SUMS_BEGIN)
             ):
-                sums.append(n_sum)
-                pieces = SUM_GROUPS[n_sum // SUMS_PER_GROUP]
+                sums.append(todo[n_sum])
+                pieces = SUM_GROUPS[todo[n_sum] // SUMS_PER_GROUP]
                 columns_summed += len(pieces) * WIDTHS[pieces[0]]
                 n_sum += 1
+            for n in tensor_sums:
+                if (step - REDLAG) * K_PASS == FIRST_COLUMN[SUM_GROUPS[n // SUMS_PER_GROUP][-1]] + WIDTHS[-1]:
+                    sums.append(n)
             if step == 0:
                 for n in sums:
                     sum_row_tile(n)
             if step < N_STEP:
                 transpose_and_group(step)
+            if step < N_PASS:
+                for n in tensor_sums:
+                    if piece_of(step * K_PASS) in SUM_GROUPS[n // SUMS_PER_GROUP]:
+                        add_blocks(n, step)
             if 0 <= step - QUANTISE_LAG < N_STEP:
                 quantise(step - QUANTISE_LAG)
             if step > 0:
@@ -265,8 +284,9 @@ def tile_probprotoseghead_k_kernel(tc, x, x_var, prototypes, proto_var, out):
                 total_sums()
             if step == SUMS_END + SPREAD + 1:
                 make_bases(proto_sums)
-            if step >= MULTIPLY_LAG:
-                multiply(step - MULTIPLY_LAG)
+            if step >= MULTIPLY_LAG and (step - MULTIPLY_LAG) % BURST == BURST - 1:
+                for s in range(step - MULTIPLY_LAG - BURST + 1, step - MULTIPLY_LAG + 1):
+                    multiply(s)
             if step == SUMS_END + SPREAD:
                 proto_sums = spread_proto_sums()
 

@@ -22,32 +22,43 @@ WORDS_PER_PASS = K_PASS // 2
 
 XV, PV, PR, X = 0, 1, 2, 3
 N_OPERANDS = 4
-LEAD = 2
-SUM_TAG, SUM_BUFS = "block_sums", 1
-ORDER = [XV, X, PV, PR]
-BANKS = {XV: 1, PV: 1, PR: 2, X: 1}
 
+ORDER = [XV, X, PV, PR]
+BANKS = {XV: 1, X: 1, PV: 1, PR: 2}
+
+LEAD = 2
 OFFSET = {XV: 0, PV: 0, PR: LEAD, X: LEAD}
 N_STEP = N_PASS + LEAD
 
-WIDTHS = [512] * 4 + [1024] * 14
-FIRST_COLUMN = [sum(WIDTHS[:i]) for i in range(len(WIDTHS))]
-N_PIECE = len(WIDTHS)
-PIECE_BUFS = 7
+VARIANCE_GROUPS = [(512, 1), (512, 1), (512, 2)] + [(1024, 2)] * 3 + [(2048, 1)] * 4
+OTHER_GROUPS = [(512, 1)] * 4 + [(1024, 1)] * 6 + [(2048, 1)] * 4
+GROUPS = {XV: VARIANCE_GROUPS, PV: VARIANCE_GROUPS, PR: OTHER_GROUPS, X: OTHER_GROUPS}
+BUFFERS = {XV: 5, PV: 5, PR: 5, X: 5}
 
 QUANTISE_LAG = 1
-BURST = 1
 MULTIPLY_LAG = 2
-SUM_GROUPS = [[0], [1], [2, 3]] + [[i, i + 1] for i in range(4, N_PIECE, 2)]
-N_GROUP = len(SUM_GROUPS)
+
 SUMS_PER_GROUP = 2 * ROW_TILES
-TENSOR_GROUPS = [3, 4, 5, 6, 7, 8]
-REDLAG = -1
+N_GROUP = len(VARIANCE_GROUPS)
+TENSOR_SUMS = {3: 0, 4: 1, 5: 2, 6: 3, 7: 0, 8: 1}
 SUMS_BEGIN, SUMS_END = 1, 31
-SPREAD = 1
 EARLY_GROUPS = 2
+SPREAD = 1
 
 FLOPS = 2 * 2 * ROWS * ROWS * D
+
+
+def width_of(i, k):
+    return GROUPS[i][k][0] * GROUPS[i][k][1]
+
+
+def first_column(i, k):
+    return sum(width_of(i, h) for h in range(k))
+
+
+def place_of(i, column):
+    k = max(k for k in range(len(GROUPS[i])) if first_column(i, k) <= column)
+    return (k,) + divmod(column - first_column(i, k), GROUPS[i][k][0])
 
 
 def tile_probprotoseghead_k_kernel(tc, x, x_var, prototypes, proto_var, out):
@@ -65,26 +76,27 @@ def tile_probprotoseghead_k_kernel(tc, x, x_var, prototypes, proto_var, out):
     out_tiles = out.rearrange("(t p) c m -> t p (c m)", p=P)
 
     with tc.tile_pool(name="const", bufs=1) as const_pool, tc.tile_pool(
-        name="natural", bufs=PIECE_BUFS
-    ) as natural_pool, tc.tile_pool(
-        name="grouped", bufs=3
-    ) as grouped_pool, tc.tile_pool(name="quantised", bufs=3) as quantised_pool, tc.tile_pool(
-        name="scratch", bufs=2
-    ) as scratch_pool, tc.tile_pool(name="tail", bufs=1) as tail_pool, tc.psum_pool(
-        name="banks", bufs=1
-    ) as bank_pool, tc.psum_pool(name="sums", bufs=1) as acc_pool, tc.manual_schedule():
+        name="natural", bufs=1
+    ) as natural_pool, tc.tile_pool(name="grouped", bufs=3) as grouped_pool, tc.tile_pool(
+        name="quantised", bufs=3
+    ) as quantised_pool, tc.tile_pool(name="scratch", bufs=2) as scratch_pool, tc.tile_pool(
+        name="tail", bufs=1
+    ) as tail_pool, tc.psum_pool(name="banks", bufs=1) as bank_pool, tc.psum_pool(
+        name="sums", bufs=1
+    ) as acc_pool, tc.manual_schedule():
         natural = {}
         grouped = {}
         codes = {}
         scales = {}
 
-        def load_piece(i, i_piece):
-            width, first = WIDTHS[i_piece], FIRST_COLUMN[i_piece]
-            natural[i, i_piece] = natural_pool.tile([P, ROW_TILES, width], BF16, name="natural%d" % i, tag="natural%d" % i)
-            nc.sync.dma_start(out=natural[i, i_piece][:], in_=sources[i][:, :, first : first + width])
-
-        def piece_of(column):
-            return max(i for i in range(N_PIECE) if FIRST_COLUMN[i] <= column)
+        def load(i, column):
+            k, n, rest = place_of(i, column)
+            width, n_load = GROUPS[i][k]
+            if n == 0:
+                natural[i, k] = natural_pool.tile(
+                    [P, n_load, ROW_TILES, width], BF16, name="natural%d" % i, tag="natural%d" % i, bufs=BUFFERS[i]
+                )
+            nc.sync.dma_start(out=natural[i, k][:, n, :, :], in_=sources[i][:, :, column : column + width])
 
         def operands_of(step):
             return [i for i in range(N_OPERANDS) if 0 <= step - OFFSET[i] < N_PASS]
@@ -95,15 +107,14 @@ def tile_probprotoseghead_k_kernel(tc, x, x_var, prototypes, proto_var, out):
             banks = {}
             for i in [i for i in ORDER if i in operands_of(step)]:
                 column = (step - OFFSET[i]) * K_PASS
-                i_piece = piece_of(column)
-                first_word = (column - FIRST_COLUMN[i_piece]) // 2
+                k, n, column_of_load = place_of(i, column)
                 banks[i] = bank_pool.tile([P, 2, ROWS], F32, name="bank%d" % i, tag="bank%d" % i, bufs=BANKS[i])
-                words = natural[i, i_piece][:].bitcast(F32)
+                words = natural[i, k][:].bitcast(F32)
                 for u in range(2):
-                    first = first_word + u * P
+                    first = column_of_load // 2 + u * P
                     for t in range(ROW_TILES):
                         nc.tensor.transpose(
-                            banks[i][:, u, t * P : (t + 1) * P], words[:, t, first : first + P], identity[:]
+                            banks[i][:, u, t * P : (t + 1) * P], words[:, n, t, first : first + P], identity[:]
                         )
             for i in operands_of(step):
                 if i in (XV, PV):
@@ -148,46 +159,48 @@ def tile_probprotoseghead_k_kernel(tc, x, x_var, prototypes, proto_var, out):
                         stop=(step == N_STEP - 1),
                     )
 
-        def sum_row_tile(n):
-            i_group, j = divmod(n, SUMS_PER_GROUP)
-            i, t = divmod(j, ROW_TILES)
-            total = partial[:, j * N_GROUP + i_group : j * N_GROUP + i_group + 1]
-            pieces = SUM_GROUPS[i_group]
-            width = WIDTHS[pieces[0]]
-            if n in tensor_sums:
-                nc.vector.tensor_reduce(out=total, in_=block_sums[n][:], axis=AXIS.X, op=ALU.add)
-            else:
-                if len(pieces) == 2:
-                    parts = [natural[i, i_piece][:, t, :] for i_piece in pieces]
-                else:
-                    parts = [natural[i, pieces[0]][:, t, h * width // 2 : (h + 1) * width // 2] for h in range(2)]
-                pair_sums = scratch_pool.tile([P, len(pieces) * width // 2], F32, name="pair_sums")
-                nc.vector.scalar_tensor_tensor(
-                    out=pair_sums[:],
-                    in0=parts[0],
-                    scalar=1.0,
-                    in1=parts[1],
-                    op0=ALU.mult,
-                    op1=ALU.add,
-                    accum_out=total,
-                )
+        def total_of(k, j):
+            return partial[:, j * N_GROUP + k : j * N_GROUP + k + 1]
 
-        def add_blocks(n, g):
-            k, j = divmod(n, SUMS_PER_GROUP)
+        def sum_row_tile(k, j):
             i, t = divmod(j, ROW_TILES)
-            i_piece = piece_of(g * K_PASS)
-            if g * K_PASS == FIRST_COLUMN[SUM_GROUPS[k][0]]:
-                block_sums[n] = bank_pool.tile([P, P], F32, name="block_sums", tag=SUM_TAG, bufs=SUM_BUFS)
+            width, n_load = VARIANCE_GROUPS[k]
+            if n_load == 1:
+                parts = natural[i, k][:, :, t, :].rearrange("p n (h c) -> p (n h) c", h=2)
+            else:
+                parts = natural[i, k][:, :, t, :]
+            half = parts.shape[1] // 2
+            pair_sums = scratch_pool.tile([P, half, parts.shape[2]], F32, name="pair_sums")
+            nc.vector.scalar_tensor_tensor(
+                out=pair_sums[:],
+                in0=parts[:, 0:half, :],
+                scalar=1.0,
+                in1=parts[:, half : 2 * half, :],
+                op0=ALU.mult,
+                op1=ALU.add,
+                accum_out=total_of(k, j),
+            )
+
+        def add_blocks(g):
+            k, n, column_of_load = place_of(XV, g * K_PASS)
+            i, t = divmod(TENSOR_SUMS[k], ROW_TILES)
+            first_pass = first_column(XV, k) // K_PASS
+            last_pass = first_pass + width_of(XV, k) // K_PASS - 1
+            if g == first_pass:
+                block_sums[k] = bank_pool.tile([P, P], F32, name="block_sums")
             for b in range(K_PASS // P):
-                first = g * K_PASS - FIRST_COLUMN[i_piece] + b * P
-                last_column = FIRST_COLUMN[i_piece] + first + P
+                first = column_of_load + b * P
                 nc.tensor.matmul(
-                    out=block_sums[n][:],
+                    out=block_sums[k][:],
                     lhsT=identity_bf16[:],
-                    rhs=natural[i, i_piece][:, t, first : first + P],
-                    start=(first + FIRST_COLUMN[i_piece] == FIRST_COLUMN[SUM_GROUPS[k][0]]),
-                    stop=(last_column == FIRST_COLUMN[SUM_GROUPS[k][-1]] + WIDTHS[SUM_GROUPS[k][-1]]),
+                    rhs=natural[i, k][:, n, t, first : first + P],
+                    start=(g == first_pass and b == 0),
+                    stop=(g == last_pass and b == K_PASS // P - 1),
                 )
+            return g == last_pass
+
+        def reduce_blocks(k):
+            nc.vector.tensor_reduce(out=total_of(k, TENSOR_SUMS[k]), in_=block_sums[k][:], axis=AXIS.X, op=ALU.add)
 
         def total_sums():
             nc.vector.tensor_reduce(
@@ -198,7 +211,7 @@ def tile_probprotoseghead_k_kernel(tc, x, x_var, prototypes, proto_var, out):
             )
 
         def spread_proto_sums():
-            proto_sums = bank_pool.tile([P, ROWS], F32, name="proto_sums", tag=SUM_TAG, bufs=SUM_BUFS)
+            proto_sums = bank_pool.tile([P, ROWS], F32, name="proto_sums", tag="block_sums")
             for t in range(ROW_TILES):
                 nc.tensor.matmul(
                     out=proto_sums[:, t * P : (t + 1) * P],
@@ -211,13 +224,8 @@ def tile_probprotoseghead_k_kernel(tc, x, x_var, prototypes, proto_var, out):
 
         def make_bases(proto_sums):
             for t in range(ROW_TILES):
-                nc.vector.tensor_scalar(
-                    out=base[t][:],
-                    in0=proto_sums[:],
-                    scalar1=-LAMDA,
-                    scalar2=row_term[:, t : t + 1],
-                    op0=ALU.mult,
-                    op1=ALU.add,
+                nc.scalar.activation(
+                    out=base[t][:], in_=proto_sums[:], func=ACT.Identity, bias=row_term[:, t : t + 1], scale=-LAMDA
                 )
 
         identity = const_pool.tile([P, P], F32, name="identity")
@@ -230,63 +238,62 @@ def tile_probprotoseghead_k_kernel(tc, x, x_var, prototypes, proto_var, out):
         base = [tail_pool.tile([P, ROWS], F32, name="base%d" % t) for t in range(ROW_TILES)]
         acc = [acc_pool.tile([P, ROWS], F32, name="acc%d" % t) for t in range(ROW_TILES)]
 
-        tensor_sums = {i_group * SUMS_PER_GROUP + i_group % SUMS_PER_GROUP for i_group in TENSOR_GROUPS}
-
-        loads = sorted(
-            ((i, i_piece) for i in range(N_OPERANDS) for i_piece in range(N_PIECE)),
-            key=lambda load: (FIRST_COLUMN[load[1]] // K_PASS + OFFSET[load[0]], ORDER.index(load[0])),
-        )
         block_sums = {}
-        todo = [n for n in range(SUMS_PER_GROUP * N_GROUP) if n not in tensor_sums]
-        all_columns = sum(len(SUM_GROUPS[n // SUMS_PER_GROUP]) * WIDTHS[SUM_GROUPS[n // SUMS_PER_GROUP][0]] for n in todo)
-        n_load = 0
+        todo = [
+            (k, j) for k in range(N_GROUP) for j in range(SUMS_PER_GROUP) if not (k in TENSOR_SUMS and TENSOR_SUMS[k] == j)
+        ]
+        all_columns = sum(width_of(XV, k) for k, j in todo)
         n_sum = 0
         columns_summed = 0
+
+        loads = []
+        for i in range(N_OPERANDS):
+            for k, (width, n_load) in enumerate(GROUPS[i]):
+                loads += [(i, first_column(i, k) + n * width) for n in range(n_load)]
+        loads.sort(key=lambda item: (item[1] // K_PASS + OFFSET[item[0]], ORDER.index(item[0])))
+        n_load = 0
+
         for step in range(N_STEP + MULTIPLY_LAG):
             while n_load < len(loads):
-                i, i_piece = loads[n_load]
-                oldest = i_piece - PIECE_BUFS
-                if oldest >= 0:
-                    i_group = [k for k in range(N_GROUP) if oldest in SUM_GROUPS[k]][0]
-                    if FIRST_COLUMN[oldest + 1] > (step - OFFSET[i]) * K_PASS:
+                i, column = loads[n_load]
+                k, n, rest = place_of(i, column)
+                oldest = k - BUFFERS[i]
+                if n == 0 and oldest >= 0:
+                    if first_column(i, oldest + 1) > (step - OFFSET[i]) * K_PASS:
                         break
-                    if i in (XV, PV) and n_sum < len(todo) and todo[n_sum] < (i_group + 1) * SUMS_PER_GROUP:
+                    if i in (XV, PV) and n_sum < len(todo) and todo[n_sum][0] <= oldest:
                         break
-                load_piece(i, i_piece)
+                load(i, column)
                 n_load += 1
+
             sums = []
             while n_sum < len(todo) and (
-                todo[n_sum] < SUMS_PER_GROUP * min(step + 1, EARLY_GROUPS)
+                todo[n_sum][0] < min(step + 1, EARLY_GROUPS)
                 or columns_summed * (SUMS_END - SUMS_BEGIN) < all_columns * (step + 1 - SUMS_BEGIN)
             ):
                 sums.append(todo[n_sum])
-                pieces = SUM_GROUPS[todo[n_sum] // SUMS_PER_GROUP]
-                columns_summed += len(pieces) * WIDTHS[pieces[0]]
+                columns_summed += width_of(XV, todo[n_sum][0])
                 n_sum += 1
-            for n in tensor_sums:
-                if (step - REDLAG) * K_PASS == FIRST_COLUMN[SUM_GROUPS[n // SUMS_PER_GROUP][-1]] + WIDTHS[-1]:
-                    sums.append(n)
             if step == 0:
-                for n in sums:
-                    sum_row_tile(n)
+                for k, j in sums:
+                    sum_row_tile(k, j)
             if step < N_STEP:
                 transpose_and_group(step)
-            if step < N_PASS:
-                for n in tensor_sums:
-                    if piece_of(step * K_PASS) in SUM_GROUPS[n // SUMS_PER_GROUP]:
-                        add_blocks(n, step)
+            group = place_of(XV, step * K_PASS)[0] if step < N_PASS else N_GROUP
+            blocks_complete = add_blocks(step) if group in TENSOR_SUMS else False
             if 0 <= step - QUANTISE_LAG < N_STEP:
                 quantise(step - QUANTISE_LAG)
             if step > 0:
-                for n in sums:
-                    sum_row_tile(n)
+                for k, j in sums:
+                    sum_row_tile(k, j)
+            if blocks_complete:
+                reduce_blocks(group)
             if step == SUMS_END:
                 total_sums()
             if step == SUMS_END + SPREAD + 1:
                 make_bases(proto_sums)
-            if step >= MULTIPLY_LAG and (step - MULTIPLY_LAG) % BURST == BURST - 1:
-                for s in range(step - MULTIPLY_LAG - BURST + 1, step - MULTIPLY_LAG + 1):
-                    multiply(s)
+            if step >= MULTIPLY_LAG:
+                multiply(step - MULTIPLY_LAG)
             if step == SUMS_END + SPREAD:
                 proto_sums = spread_proto_sums()
 

@@ -30,10 +30,10 @@ LEAD = 2
 OFFSET = {XV: 0, PV: 0, PR: LEAD, X: LEAD}
 N_STEP = N_PASS + LEAD
 
-VARIANCE_GROUPS = [(512, 1), (512, 1), (512, 2)] + [(1024, 2)] * 3 + [(2048, 1)] * 4
-OTHER_GROUPS = [(512, 1)] * 4 + [(1024, 1)] * 6 + [(2048, 1)] * 4
+VARIANCE_GROUPS = [(512, 1), (512, 1), (512, 2)] + [(1024, 2)] * 7
+OTHER_GROUPS = [(512, 1)] * 4 + [(1024, 1)] * 14
 GROUPS = {XV: VARIANCE_GROUPS, PV: VARIANCE_GROUPS, PR: OTHER_GROUPS, X: OTHER_GROUPS}
-BUFFERS = {XV: 5, PV: 5, PR: 5, X: 5}
+BUFFERS = {XV: 5, PV: 5, PR: 7, X: 7}
 
 QUANTISE_LAG = 1
 MULTIPLY_LAG = 2

@@ -30,8 +30,8 @@ LEAD = 2
 OFFSET = {XV: 0, PV: 0, PR: LEAD, X: LEAD}
 N_STEP = N_PASS + LEAD
 
-VARIANCE_GROUPS = [(512, 1), (512, 1), (512, 2)] + [(1024, 2)] * 7
-OTHER_GROUPS = [(512, 1)] * 4 + [(1024, 1)] * 14
+VARIANCE_GROUPS = [(512, 1), (512, 1), (512, 2), (512, 4)] + [(1024, 2)] * 6
+OTHER_GROUPS = [(512, 1)] * 8 + [(1024, 1)] * 12
 GROUPS = {XV: VARIANCE_GROUPS, PV: VARIANCE_GROUPS, PR: OTHER_GROUPS, X: OTHER_GROUPS}
 BUFFERS = {XV: 5, PV: 5, PR: 7, X: 7}
 
@@ -40,7 +40,7 @@ MULTIPLY_LAG = 2
 
 SUMS_PER_GROUP = 2 * ROW_TILES
 N_GROUP = len(VARIANCE_GROUPS)
-TENSOR_SUMS = {3: 0, 4: 1, 5: 2, 6: 3, 7: 0, 8: 1}
+TENSOR_SUMS = {3: 0, 4: 0, 5: 0, 6: 1, 7: 1, 8: 1}
 SUMS_BEGIN, SUMS_END = 1, 31
 EARLY_GROUPS = 2
 SPREAD = 1
@@ -183,15 +183,17 @@ def tile_probprotoseghead_k_kernel(tc, x, x_var, prototypes, proto_var, out):
 
         def add_blocks(g):
             k, n, column_of_load = place_of(XV, g * K_PASS)
-            i, t = divmod(TENSOR_SUMS[k], ROW_TILES)
-            first_pass = first_column(XV, k) // K_PASS
-            last_pass = first_pass + width_of(XV, k) // K_PASS - 1
+            j = TENSOR_SUMS[k]
+            i, t = divmod(j, ROW_TILES)
+            run = [h for h in TENSOR_SUMS if TENSOR_SUMS[h] == j]
+            first_pass = first_column(XV, run[0]) // K_PASS
+            last_pass = first_column(XV, run[-1] + 1) // K_PASS - 1
             if g == first_pass:
-                block_sums[k] = bank_pool.tile([P, P], F32, name="block_sums")
+                block_sums[j] = bank_pool.tile([P, P], F32, name="block_sums")
             for b in range(K_PASS // P):
                 first = column_of_load + b * P
                 nc.tensor.matmul(
-                    out=block_sums[k][:],
+                    out=block_sums[j][:],
                     lhsT=identity_bf16[:],
                     rhs=natural[i, k][:, n, t, first : first + P],
                     start=(g == first_pass and b == 0),
@@ -200,7 +202,7 @@ def tile_probprotoseghead_k_kernel(tc, x, x_var, prototypes, proto_var, out):
             return g == last_pass
 
         def reduce_blocks(k):
-            nc.vector.tensor_reduce(out=total_of(k, TENSOR_SUMS[k]), in_=block_sums[k][:], axis=AXIS.X, op=ALU.add)
+            nc.vector.tensor_reduce(out=total_of(k, TENSOR_SUMS[k]), in_=block_sums[TENSOR_SUMS[k]][:], axis=AXIS.X, op=ALU.add)
 
         def total_sums():
             nc.vector.tensor_reduce(
@@ -233,6 +235,7 @@ def tile_probprotoseghead_k_kernel(tc, x, x_var, prototypes, proto_var, out):
         identity_bf16 = const_pool.tile([P, P], BF16, name="identity_bf16")
         make_identity(nc, identity_bf16[:])
         partial = const_pool.tile([P, SUMS_PER_GROUP * N_GROUP], F32, name="partial")
+        nc.gpsimd.memset(partial[:], 0.0)
         totals = tail_pool.tile([P, 2 * ROW_TILES], F32, name="totals")
         row_term = tail_pool.tile([P, ROW_TILES], F32, name="row_term")
         base = [tail_pool.tile([P, ROWS], F32, name="base%d" % t) for t in range(ROW_TILES)]

@@ -40,7 +40,7 @@ MULTIPLY_LAG = 2
 
 SUMS_PER_GROUP = 2 * ROW_TILES
 N_GROUP = len(VARIANCE_GROUPS)
-TENSOR_SUMS = {3: 0, 4: 0, 5: 0, 6: 1, 7: 1, 8: 1}
+TENSOR_SUMS = {4: 0, 5: 0, 6: 0, 7: 1, 8: 1, 9: 1}
 SUMS_BEGIN, SUMS_END = 1, 31
 EARLY_GROUPS = 2
 SPREAD = 1

@@ -26,12 +26,12 @@ N_OPERANDS = 4
 ORDER = [XV, X, PV, PR]
 BANKS = {XV: 1, X: 1, PV: 1, PR: 2}
 
-LEAD = 2
+LEAD = 1
 OFFSET = {XV: 0, PV: 0, PR: LEAD, X: LEAD}
 N_STEP = N_PASS + LEAD
 
-VARIANCE_GROUPS = [(512, 1), (512, 1), (512, 2), (512, 4)] + [(1024, 2)] * 6
-OTHER_GROUPS = [(512, 1)] * 8 + [(1024, 1)] * 12
+VARIANCE_GROUPS = [(1024, 1)] * 2 + [(1024, 2)] * 7
+OTHER_GROUPS = [(1024, 1)] * 16
 GROUPS = {XV: VARIANCE_GROUPS, PV: VARIANCE_GROUPS, PR: OTHER_GROUPS, X: OTHER_GROUPS}
 BUFFERS = {XV: 5, PV: 5, PR: 7, X: 7}
 
@@ -40,9 +40,9 @@ MULTIPLY_LAG = 2
 
 SUMS_PER_GROUP = 2 * ROW_TILES
 N_GROUP = len(VARIANCE_GROUPS)
-TENSOR_SUMS = {4: 0, 5: 0, 6: 0, 7: 1, 8: 1, 9: 1}
+TENSOR_SUMS = {3: 0, 4: 0, 5: 0, 6: 1, 7: 1, 8: 1}
 SUMS_BEGIN, SUMS_END = 1, 31
-EARLY_GROUPS = 2
+EARLY_GROUPS = 1
 SPREAD = 1
 
 FLOPS = 2 * 2 * ROWS * ROWS * D

import concourse.mybir as mybir
from concourse.masks import make_identity

F32 = mybir.dt.float32
BF16 = mybir.dt.bfloat16
U32 = mybir.dt.uint32
U8 = mybir.dt.uint8
FP8X4 = mybir.dt.float8_e4m3fn_x4
ACT = mybir.ActivationFunctionType
ALU = mybir.AluOpType
AXIS = mybir.AxisListType

P = 128
ROWS = 256
ROW_TILES = ROWS // P
D = 16384
LAMDA = 1.0 / D
ROOT_SCALE = 2.0**-14
K_PASS = 4 * P
N_PASS = D // K_PASS
WORDS_PER_PASS = K_PASS // 2

XV, PV, PR, X = 0, 1, 2, 3
N_OPERANDS = 4

ORDER = [XV, X, PV, PR]
BANKS = {XV: 1, X: 1, PV: 1, PR: 2}

LEAD = 1
OFFSET = {XV: 0, PV: 0, PR: LEAD, X: LEAD}
N_STEP = N_PASS + LEAD

VARIANCE_GROUPS = [(1024, 1)] * 2 + [(1024, 2)] * 7
OTHER_GROUPS = [(1024, 1)] * 16
GROUPS = {XV: VARIANCE_GROUPS, PV: VARIANCE_GROUPS, PR: OTHER_GROUPS, X: OTHER_GROUPS}
BUFFERS = {XV: 5, PV: 5, PR: 7, X: 7}

QUANTISE_LAG = 1
MULTIPLY_LAG = 2

SUMS_PER_GROUP = 2 * ROW_TILES
N_GROUP = len(VARIANCE_GROUPS)
TENSOR_SUMS = {3: 0, 4: 0, 5: 0, 6: 1, 7: 1, 8: 1}
SUMS_BEGIN, SUMS_END = 1, 31
EARLY_GROUPS = 1
SPREAD = 1

FLOPS = 2 * 2 * ROWS * ROWS * D


def width_of(i, k):
    return GROUPS[i][k][0] * GROUPS[i][k][1]


def first_column(i, k):
    return sum(width_of(i, h) for h in range(k))


def place_of(i, column):
    k = max(k for k in range(len(GROUPS[i])) if first_column(i, k) <= column)
    return (k,) + divmod(column - first_column(i, k), GROUPS[i][k][0])


def tile_probprotoseghead_k_kernel(tc, x, x_var, prototypes, proto_var, out):
    nc = tc.nc

    def row_tiled(ap):
        return ap.rearrange("(t p) d -> p t d", p=P)

    sources = {
        XV: row_tiled(x_var),
        PV: row_tiled(proto_var.rearrange("c m d -> (c m) d")),
        PR: row_tiled(prototypes.rearrange("c m d -> (c m) d")),
        X: row_tiled(x),
    }
    out_tiles = out.rearrange("(t p) c m -> t p (c m)", p=P)

    with tc.tile_pool(name="const", bufs=1) as const_pool, tc.tile_pool(
        name="natural", bufs=1
    ) as natural_pool, tc.tile_pool(name="grouped", bufs=3) as grouped_pool, tc.tile_pool(
        name="quantised", bufs=3
    ) as quantised_pool, tc.tile_pool(name="scratch", bufs=2) as scratch_pool, tc.tile_pool(
        name="tail", bufs=1
    ) as tail_pool, tc.psum_pool(name="banks", bufs=1) as bank_pool, tc.psum_pool(
        name="sums", bufs=1
    ) as acc_pool, tc.manual_schedule():
        natural = {}
        grouped = {}
        codes = {}
        scales = {}

        def load(i, column):
            k, n, rest = place_of(i, column)
            width, n_load = GROUPS[i][k]
            if n == 0:
                natural[i, k] = natural_pool.tile(
                    [P, n_load, ROW_TILES, width], BF16, name="natural%d" % i, tag="natural%d" % i, bufs=BUFFERS[i]
                )
            nc.sync.dma_start(out=natural[i, k][:, n, :, :], in_=sources[i][:, :, column : column + width])

        def operands_of(step):
            return [i for i in range(N_OPERANDS) if 0 <= step - OFFSET[i] < N_PASS]

        def transpose_and_group(step):
            grouped[step] = grouped_pool.tile([P, N_OPERANDS, 4 * ROWS], BF16, name="grouped", align_bytes=64)
            grouped_words = grouped[step][:].bitcast(F32)
            banks = {}
            for i in [i for i in ORDER if i in operands_of(step)]:
                column = (step - OFFSET[i]) * K_PASS
                k, n, column_of_load = place_of(i, column)
                banks[i] = bank_pool.tile([P, 2, ROWS], F32, name="bank%d" % i, tag="bank%d" % i, bufs=BANKS[i])
                words = natural[i, k][:].bitcast(F32)
                for u in range(2):
                    first = column_of_load // 2 + u * P
                    for t in range(ROW_TILES):
                        nc.tensor.transpose(
                            banks[i][:, u, t * P : (t + 1) * P], words[:, n, t, first : first + P], identity[:]
                        )
            for i in operands_of(step):
                if i in (XV, PV):
                    nc.scalar.activation(
                        out=grouped[step][:, i, :].rearrange("p (r u e) -> p r u e", u=2, e=2),
                        in_=banks[i][:].bitcast(BF16).rearrange("p u (r e) -> p r u e", e=2),
                        func=ACT.Sqrt,
                        scale=ROOT_SCALE,
                    )
                else:
                    copy = nc.scalar.copy if i == PR else nc.vector.tensor_copy
                    copy(
                        out=grouped_words[:, i, :].rearrange("p (r u) -> p r u", u=2),
                        in_=banks[i][:].rearrange("p u r -> p r u"),
                    )

        def quantise(step):
            codes[step] = quantised_pool.tile([P, N_OPERANDS * ROWS], U32, name="codes", align_bytes=64)
            scales[step] = quantised_pool.tile([P, N_OPERANDS * ROWS], U8, name="scales", align_bytes=64)
            first, last = operands_of(step)[0], operands_of(step)[-1]
            words = slice(first * ROWS, (last + 1) * ROWS)
            nc.vector.quantize_mx(
                out=codes[step][:, words].bitcast(FP8X4),
                scales=scales[step][:, words],
                in_=grouped[step][:, first : last + 1, :].rearrange("p i c -> p (i c)"),
            )

        def multiply(step):
            for rows_of, columns_of in ((XV, PV), (X, PR)):
                if rows_of not in operands_of(step):
                    continue
                moving = slice(columns_of * ROWS, (columns_of + 1) * ROWS)
                for t in range(ROW_TILES):
                    stationary = slice(rows_of * ROWS + t * P, rows_of * ROWS + (t + 1) * P)
                    nc.tensor.matmul_mx(
                        out=acc[t][:],
                        lhsT=codes[step][:, stationary].bitcast(FP8X4),
                        lhsT_scale=scales[step][:, stationary],
                        rhs=codes[step][:, moving].bitcast(FP8X4),
                        rhs_scale=scales[step][:, moving],
                        start=(step == 0),
                        stop=(step == N_STEP - 1),
                    )

        def total_of(k, j):
            return partial[:, j * N_GROUP + k : j * N_GROUP + k + 1]

        def sum_row_tile(k, j):
            i, t = divmod(j, ROW_TILES)
            width, n_load = VARIANCE_GROUPS[k]
            if n_load == 1:
                parts = natural[i, k][:, :, t, :].rearrange("p n (h c) -> p (n h) c", h=2)
            else:
                parts = natural[i, k][:, :, t, :]
            half = parts.shape[1] // 2
            pair_sums = scratch_pool.tile([P, half, parts.shape[2]], F32, name="pair_sums")
            nc.vector.scalar_tensor_tensor(
                out=pair_sums[:],
                in0=parts[:, 0:half, :],
                scalar=1.0,
                in1=parts[:, half : 2 * half, :],
                op0=ALU.mult,
                op1=ALU.add,
                accum_out=total_of(k, j),
            )

        def add_blocks(g):
            k, n, column_of_load = place_of(XV, g * K_PASS)
            j = TENSOR_SUMS[k]
            i, t = divmod(j, ROW_TILES)
            run = [h for h in TENSOR_SUMS if TENSOR_SUMS[h] == j]
            first_pass = first_column(XV, run[0]) // K_PASS
            last_pass = first_column(XV, run[-1] + 1) // K_PASS - 1
            if g == first_pass:
                block_sums[j] = bank_pool.tile([P, P], F32, name="block_sums")
            for b in range(K_PASS // P):
                first = column_of_load + b * P
                nc.tensor.matmul(
                    out=block_sums[j][:],
                    lhsT=identity_bf16[:],
                    rhs=natural[i, k][:, n, t, first : first + P],
                    start=(g == first_pass and b == 0),
                    stop=(g == last_pass and b == K_PASS // P - 1),
                )
            return g == last_pass

        def reduce_blocks(k):
            nc.vector.tensor_reduce(out=total_of(k, TENSOR_SUMS[k]), in_=block_sums[TENSOR_SUMS[k]][:], axis=AXIS.X, op=ALU.add)

        def total_sums():
            nc.vector.tensor_reduce(
                out=totals[:], in_=partial[:].rearrange("p (j c) -> p j c", c=N_GROUP), axis=AXIS.X, op=ALU.add
            )
            nc.vector.tensor_scalar(
                out=row_term[:], in0=totals[:, 0:ROW_TILES], scalar1=-LAMDA, scalar2=-2.0, op0=ALU.mult, op1=ALU.add
            )

        def spread_proto_sums():
            proto_sums = bank_pool.tile([P, ROWS], F32, name="proto_sums", tag="block_sums")
            for t in range(ROW_TILES):
                nc.tensor.matmul(
                    out=proto_sums[:, t * P : (t + 1) * P],
                    lhsT=totals[:, ROW_TILES + t : ROW_TILES + t + 1].to_broadcast([P, P]),
                    rhs=identity[:],
                    start=True,
                    stop=True,
                )
            return proto_sums

        def make_bases(proto_sums):
            for t in range(ROW_TILES):
                nc.scalar.activation(
                    out=base[t][:], in_=proto_sums[:], func=ACT.Identity, bias=row_term[:, t : t + 1], scale=-LAMDA
                )

        identity = const_pool.tile([P, P], F32, name="identity")
        make_identity(nc, identity[:])
        identity_bf16 = const_pool.tile([P, P], BF16, name="identity_bf16")
        make_identity(nc, identity_bf16[:])
        partial = const_pool.tile([P, SUMS_PER_GROUP * N_GROUP], F32, name="partial")
        nc.gpsimd.memset(partial[:], 0.0)
        totals = tail_pool.tile([P, 2 * ROW_TILES], F32, name="totals")
        row_term = tail_pool.tile([P, ROW_TILES], F32, name="row_term")
        base = [tail_pool.tile([P, ROWS], F32, name="base%d" % t) for t in range(ROW_TILES)]
        acc = [acc_pool.tile([P, ROWS], F32, name="acc%d" % t) for t in range(ROW_TILES)]

        block_sums = {}
        todo = [
            (k, j) for k in range(N_GROUP) for j in range(SUMS_PER_GROUP) if not (k in TENSOR_SUMS and TENSOR_SUMS[k] == j)
        ]
        all_columns = sum(width_of(XV, k) for k, j in todo)
        n_sum = 0
        columns_summed = 0

        loads = []
        for i in range(N_OPERANDS):
            for k, (width, n_load) in enumerate(GROUPS[i]):
                loads += [(i, first_column(i, k) + n * width) for n in range(n_load)]
        loads.sort(key=lambda item: (item[1] // K_PASS + OFFSET[item[0]], ORDER.index(item[0])))
        n_load = 0

        for step in range(N_STEP + MULTIPLY_LAG):
            while n_load < len(loads):
                i, column = loads[n_load]
                k, n, rest = place_of(i, column)
                oldest = k - BUFFERS[i]
                if n == 0 and oldest >= 0:
                    if first_column(i, oldest + 1) > (step - OFFSET[i]) * K_PASS:
                        break
                    if i in (XV, PV) and n_sum < len(todo) and todo[n_sum][0] <= oldest:
                        break
                load(i, column)
                n_load += 1

            sums = []
            while n_sum < len(todo) and (
                todo[n_sum][0] < min(step + 1, EARLY_GROUPS)
                or columns_summed * (SUMS_END - SUMS_BEGIN) < all_columns * (step + 1 - SUMS_BEGIN)
            ):
                sums.append(todo[n_sum])
                columns_summed += width_of(XV, todo[n_sum][0])
                n_sum += 1
            if step == 0:
                for k, j in sums:
                    sum_row_tile(k, j)
            if step < N_STEP:
                transpose_and_group(step)
            group = place_of(XV, step * K_PASS)[0] if step < N_PASS else N_GROUP
            blocks_complete = add_blocks(step) if group in TENSOR_SUMS else False
            if 0 <= step - QUANTISE_LAG < N_STEP:
                quantise(step - QUANTISE_LAG)
            if step > 0:
                for k, j in sums:
                    sum_row_tile(k, j)
            if blocks_complete:
                reduce_blocks(group)
            if step == SUMS_END:
                total_sums()
            if step == SUMS_END + SPREAD + 1:
                make_bases(proto_sums)
            if step >= MULTIPLY_LAG:
                multiply(step - MULTIPLY_LAG)
            if step == SUMS_END + SPREAD:
                proto_sums = spread_proto_sums()

        for t in range(ROW_TILES):
            result = tail_pool.tile([P, ROWS], F32, name="result%d" % t)
            nc.vector.scalar_tensor_tensor(
                out=result[:], in0=acc[t][:], scalar=2.0, in1=base[t][:], op0=ALU.mult, op1=ALU.add
            )
            nc.sync.dma_start(out=out_tiles[t], in_=result[:])
